import numpy as np
import ml_dtypes


def mxq(x, axis, fmt="e4m3"):
    dtype, down = {"e4m3": (ml_dtypes.float8_e4m3fn, 7), "e5m2": (ml_dtypes.float8_e5m2, 14)}[fmt]
    v = np.moveaxis(np.asarray(x, np.float32).astype(ml_dtypes.bfloat16).astype(np.float64), axis, -1)
    blocks = v.reshape(v.shape[:-1] + (-1, 32))
    amax = np.abs(blocks).max(-1, keepdims=True)
    byte = np.maximum(np.where(amax > 0, np.frexp(amax)[1] - 1 + 127, 0) - down, 1)
    scale = np.exp2(byte - 127.0)
    codes = (blocks / scale).astype(np.float32).astype(dtype).astype(np.float64)
    return np.moveaxis((codes * scale).reshape(v.shape), -1, axis)


WIDE = False


def mx_kscale(k):
    if not WIDE:
        return np.ones(k)
    levels = np.array([10, -10, 5, -5, 0])
    if k % 512:
        return np.exp2(np.random.permutation(np.resize(levels, k // 32))).repeat(32)
    a = np.empty((k // 512, 16))
    for p in range(k // 512):
        a[p, :8] = np.random.permutation(np.resize(levels, 8))
        for g in range(8):
            far = levels[np.abs(levels - a[p, g]) >= 10]
            a[p, g + 8] = far[np.random.randint(len(far))]
    return np.exp2(a.ravel()).repeat(32)


BF16 = ml_dtypes.bfloat16


def bf(x):
    return np.asarray(x, np.float32).astype(BF16)


def f64(x):
    return np.asarray(x).astype(np.float64)


B, I, O, C, L = 8, 1024, 128, 4, 8
EDGES = min(L * int(np.lcm(I, O)), I * O)
KO = EDGES // O
KI = EDGES // I
SIGN = 1


def make_mask():
    cols = np.repeat(np.arange(I), KI)
    np.random.shuffle(cols)
    cols = cols.reshape(O, KO)
    m = np.zeros((O, I))
    m[np.arange(O)[:, None], cols] = 1.0
    return m


def setup_inputs():
    s = mx_kscale(I)
    g = np.exp2(np.round(np.log2(s.mean())))
    a = np.random.standard_normal((B, I, I))
    a[:, np.arange(I), np.arange(I)] *= 8.0
    a = a * (KO / 4.0) * (g * g) / s[:, None] / s[None, :]
    return {"input": bf(a), "mask": bf(make_mask()), "weight": bf(np.random.random_sample((C, O, I)) * (3.0 / KO) * s)}


def reference(input, mask, weight):
    compressor = f64(mask) * f64(weight)
    inp = f64(input)
    inp = inp * (1.0 - np.eye(inp.shape[-1]))
    cq = mxq(compressor, 2, "e4m3")
    tmp = cq[None] @ mxq(inp, 1, "e4m3")[:, None]
    out = mxq(tmp, 3, "e4m3") @ cq.transpose(0, 2, 1)[None]
    rs = compressor.sum(-1)
    norm = rs[:, :, None] * rs[:, None, :]
    out = out / np.where(norm == 0, np.ones_like(norm), norm)
    out = SIGN * out
    return out.reshape(B * C, O, O)

@@ -1,0 +1,341 @@
+from contextlib import ExitStack
+
+import concourse.mybir as mybir
+from concourse.masks import make_identity
+
+F32 = mybir.dt.float32
+BF16 = mybir.dt.bfloat16
+U32 = mybir.dt.uint32
+U8 = mybir.dt.uint8
+FP8X4 = mybir.dt.float8_e4m3fn_x4
+ALU = mybir.AluOpType
+
+P = 128
+B, I, O, C = 8, 1024, 128, 4
+H = I // 2
+NCH = 2 * B
+FLOPS = 2 * B * C * O * I * I + 2 * B * C * O * I * O
+
+PIN = False
+SCOLS = [512,512,512,512,416,416,416,416,416,416,416,416,416,416,352,288]
+RAWB = 4
+JH = 3
+XE_V = (7,)
+TQ_LAG = 4
+F_LAG = 5
+ST_ENG = "sync"
+PITCH = I + 12
+GP = 4 * PITCH
+DIAG = 4 * (PITCH + 4)
+RAWLEN = GP + H + DIAG
+
+
+def tile_verticalcompression_t_kernel(tc, a_in, mask, weight, out):
+    nc = tc.nc
+    with ExitStack() as ctx:
+        const = ctx.enter_context(tc.tile_pool(name="const", bufs=1))
+        rawp = ctx.enter_context(tc.tile_pool(name="rawp", bufs=RAWB))
+        grpp = ctx.enter_context(tc.tile_pool(name="grpp", bufs=4))
+        acp = ctx.enter_context(tc.tile_pool(name="acp", bufs=4))
+        tgp = ctx.enter_context(tc.tile_pool(name="tgp", bufs=4))
+        tcp = ctx.enter_context(tc.tile_pool(name="tcp", bufs=6))
+        outp = ctx.enter_context(tc.tile_pool(name="outp", bufs=3))
+        ps1 = ctx.enter_context(tc.psum_pool(name="ps1", bufs=7))
+        ps2 = ctx.enter_context(tc.psum_pool(name="ps2", bufs=1))
+        if PIN:
+            ctx.enter_context(tc.manual_schedule())
+
+        raws = {}
+        grps = {}
+        acs = {}
+        banks = {}
+        tgs = {}
+        tcs = {}
+        banks2 = {}
+
+        def raw_rows(b, g):
+            return raws[b][:, GP * g : GP * (g + 1)].rearrange("p (j w) -> p j w", w=PITCH)
+
+        def load(b):
+            raw = rawp.tile([P, RAWLEN], BF16, tag="raw", name="raw")
+            raws[b] = raw
+            for h in range(2):
+                for g in range(2) if b < JH else [h]:
+                    cols = slice(H * h, H * (h + 1)) if b < JH else slice(0, I)
+                    rows = a_in[b, H * g : H * (g + 1), cols].rearrange("(q j s) w -> s q j w", j=4, s=4)
+                    for s in range(4):
+                        nc.sync.dma_start(
+                            out=raw[s:P:4, GP * g : GP * (g + 1)].rearrange("p (j w) -> p j w", w=PITCH)[:, :, cols],
+                            in_=rows[s],
+                        )
+
+        mask_sb = const.tile([P, I], BF16, name="mask_sb")
+        nc.sync.dma_start(out=mask_sb[:], in_=mask)
+        w_sb = const.tile([P, C, I], BF16, name="w_sb")
+        for c in range(C):
+            nc.sync.dma_start(out=w_sb[:, c, :], in_=weight[c])
+        for b in range(RAWB):
+            load(b)
+
+        ident = const.tile([P, P], BF16, name="ident")
+        make_identity(nc, ident[:])
+        identf = const.tile([P, P], F32, name="identf")
+        make_identity(nc, identf[:])
+        noti = const.tile([P, P], BF16, name="noti")
+        nc.vector.tensor_scalar(
+            out=noti[:], in0=ident[:], scalar1=-1.0, scalar2=1.0, op0=ALU.mult, op1=ALU.add
+        )
+
+        comp = const.tile([P, C, 4, I // 4], BF16, name="comp")
+        cg = const.tile([P, 2, C, P, 4], BF16, name="cg", align_bytes=64)
+        ccodes = const.tile([P, 2, C, P], U32, name="ccodes", align_bytes=64)
+        cscales = const.tile([P, 2, C, P], U8, name="cscales", align_bytes=64)
+        rs = const.tile([P, C], F32, name="rs")
+        ones = const.tile([P, 32], BF16, name="ones")
+        nc.gpsimd.memset(ones[:], 1.0)
+        rsbs = {}
+        inv = const.tile([P, C, P], F32, name="inv")
+        for c in range(C):
+            nc.vector.tensor_tensor(
+                out=comp[:, c, :, :].rearrange("p t (x s) -> p t x s", s=4),
+                in0=w_sb[:, c, :].rearrange("p (x t s) -> p t x s", t=4, s=4),
+                in1=mask_sb[:].rearrange("p (x t s) -> p t x s", t=4, s=4),
+                op=ALU.mult,
+            )
+        for c in range(C):
+            for g in range(2):
+                xt = ps1.tile([P, 4, P], BF16, tag="s1", name="xt")
+                for t in range(4):
+                    nc.tensor.transpose(xt[:, t, :], comp[:, c, t, P * g : P * (g + 1)], ident[:])
+                fn = nc.vector.tensor_copy if 2 * c + g in XE_V else nc.scalar.copy
+                fn(out=cg[:, g, c, :, :], in_=xt[:].rearrange("p t o -> p o t"))
+
+        def quant_comp():
+            nc.vector.quantize_mx(
+                out=ccodes[:].rearrange("p g c o -> p (g c o)").bitcast(FP8X4),
+                scales=cscales[:].rearrange("p g c o -> p (g c o)"),
+                in_=cg[:].rearrange("p g c o t -> p (g c o t)"),
+            )
+
+        def row_mass(c):
+            if c == 0:
+                rsbs[0] = ps2.tile([P, C, 32], F32, tag="s2", name="rsb")
+            for i in range(8):
+                nc.tensor.matmul(
+                    out=rsbs[0][:, c, :],
+                    lhsT=cg[:, i // 4, c, :, i % 4],
+                    rhs=ones[:],
+                    start=(i == 0),
+                    stop=(i == 7),
+                )
+
+        safe = const.tile([P, C], F32, name="safe")
+        rec = const.tile([P, C], F32, name="rec")
+        rp = const.tile([P, C], F32, name="rp")
+        spread = const.tile([P, C, P], F32, name="spread")
+        prod = const.tile([P, C, P], F32, name="prod")
+
+        def inv_rs():
+            nc.vector.tensor_copy(out=rs[:], in_=rsbs[0][:, :, 0])
+
+        def inv_safe():
+            nc.vector.scalar_tensor_tensor(
+                out=safe[:], in0=rs[:], scalar=0.0, in1=rs[:], op0=ALU.is_equal, op1=ALU.add
+            )
+
+        def inv_rec():
+            nc.vector.reciprocal(out=rec[:], in_=safe[:])
+
+        def inv_rp():
+            nc.vector.scalar_tensor_tensor(
+                out=rp[:], in0=rs[:], scalar=0.0, in1=rec[:], op0=ALU.not_equal, op1=ALU.mult
+            )
+
+        def inv_spread():
+            nc.vector.tensor_copy(out=spread[:], in_=rp[:].unsqueeze(2).to_broadcast([P, C, P]))
+            rsbs[1] = ps2.tile([P, C, P], F32, tag="s2", name="rb")
+            for c in range(C):
+                nc.tensor.transpose(rsbs[1][:, c, :], spread[:, c, :], identf[:])
+
+        def inv_prod():
+            nc.vector.tensor_tensor(
+                out=prod[:], in0=rsbs[1][:], in1=rp[:].unsqueeze(2).to_broadcast([P, C, P]), op=ALU.mult
+            )
+
+        def inv_fix():
+            nc.vector.scalar_tensor_tensor(
+                out=inv[:].rearrange("p c o -> p (c o)"),
+                in0=prod[:].rearrange("p c o -> p (c o)"),
+                scalar=0.0,
+                in1=prod[:].rearrange("p c o -> p (c o)"),
+                op0=ALU.is_equal,
+                op1=ALU.add,
+            )
+
+        inv_steps = [inv_rs, inv_safe, inv_rec, inv_rp, inv_spread, inv_prod, inv_fix]
+
+        def inv_step(i):
+            if 0 <= i < len(inv_steps):
+                inv_steps[i]()
+
+        def zero_diag(b, g):
+            d0 = GP * g + H * g
+            blocks = raws[b][:, d0 : d0 + DIAG].rearrange("p (j u z) -> p j u z", j=4, z=16)[:, :, 0:32, 0:4]
+            nc.vector.tensor_tensor(
+                out=blocks,
+                in0=blocks,
+                in1=noti[:].rearrange("p (q s) -> p q s", s=4).unsqueeze(1).to_broadcast([P, 4, 32, 4]),
+                op=ALU.mult,
+            )
+
+        def regroup(fn, n, g, q0, q1):
+            b, gj = divmod(n, 2)
+            fn(
+                out=grps[n][:, g, :, 4 * q0 : 4 * q1, :].rearrange("p t (q s) j -> p q t j s", s=4),
+                in_=raw_rows(b, g)[:, :, H * gj + 16 * q0 : H * gj + 16 * q1].rearrange(
+                    "p j (q t s) -> p q t j s", t=4, s=4
+                ),
+            )
+
+        def front_m(n):
+            zero_diag(n // 2, n % 2)
+
+        def front_v(n):
+            b, gj = divmod(n, 2)
+            grps[n] = grpp.tile([P, 2, 4, P, 4], BF16, tag="grp", name="grp", align_bytes=64)
+            regroup(nc.vector.tensor_copy, n, gj, 0, 32)
+            if SCOLS[n] < H:
+                regroup(nc.vector.tensor_copy, n, 1 - gj, 0, (H - SCOLS[n]) // 16)
+
+        def front_s(n, piece):
+            gj = n % 2
+            if piece == 0:
+                regroup(nc.scalar.copy, n, 1 - gj, (H - SCOLS[n]) // 16, 32)
+
+        def quant_a(n):
+            codes = acp.tile([P, 2, H], U32, tag="ac", name="ac", align_bytes=64)
+            scl = acp.tile([P, 2, H], U8, tag="asc", name="asc", align_bytes=64)
+            nc.vector.quantize_mx(
+                out=codes[:].rearrange("p g w -> p (g w)").bitcast(FP8X4),
+                scales=scl[:].rearrange("p g w -> p (g w)"),
+                in_=grps[n][:].rearrange("p g t m j -> p (g t m j)"),
+            )
+            acs[n] = (codes, scl)
+
+        def stage1(n, c):
+            codes, scl = acs[n]
+            bank = ps1.tile([P, 4, P], F32, tag="s1", name="bank")
+            for t in range(4):
+                for g in range(2):
+                    nc.tensor.matmul_mx(
+                        out=bank[:, t, :],
+                        lhsT=codes[:, g, P * t : P * (t + 1)].bitcast(FP8X4),
+                        lhsT_scale=scl[:, g, P * t : P * (t + 1)],
+                        rhs=ccodes[:, g, c, :].bitcast(FP8X4),
+                        rhs_scale=cscales[:, g, c, :],
+                        start=(g == 0),
+                        stop=(g == 1),
+                    )
+            banks[(n, c)] = bank
+
+        def evac(fn, n, c):
+            if c == 0:
+                tgs[n] = tgp.tile([P, C, P, 4], BF16, tag="tg", name="tg", align_bytes=64)
+            fn(out=tgs[n][:, c, :, :], in_=banks[(n, c)][:].rearrange("p t o -> p o t"))
+
+        def quant_t(n, c0, c1):
+            if c0 == 0:
+                tcs[n] = (
+                    tcp.tile([P, C, P], U32, tag="tcod", name="tcod", align_bytes=64),
+                    tcp.tile([P, C, P], U8, tag="tscl", name="tscl", align_bytes=64),
+                )
+            tcod, tscl = tcs[n]
+            nc.vector.quantize_mx(
+                out=tcod[:, c0:c1, :].rearrange("p c o -> p (c o)").bitcast(FP8X4),
+                scales=tscl[:, c0:c1, :].rearrange("p c o -> p (c o)"),
+                in_=tgs[n][:, c0:c1, :, :].rearrange("p c o t -> p (c o t)"),
+            )
+
+        def stage2(b, c0, c1):
+            if c0 == 0:
+                banks2[b] = ps2.tile([P, C, P], F32, tag="s2", name="bank2")
+            for c in range(c0, c1):
+                for gj in range(2):
+                    tcod, tscl = tcs[2 * b + gj]
+                    nc.tensor.matmul_mx(
+                        out=banks2[b][:, c, :],
+                        lhsT=tcod[:, c, :].bitcast(FP8X4),
+                        lhsT_scale=tscl[:, c, :],
+                        rhs=ccodes[:, gj, c, :].bitcast(FP8X4),
+                        rhs_scale=cscales[:, gj, c, :],
+                        start=(gj == 0),
+                        stop=(gj == 1),
+                    )
+
+        def final(b, c0, c1):
+            osb = outp.tile([P, c1 - c0, P], F32, tag="osb", name="osb")
+            nc.vector.tensor_tensor(out=osb[:], in0=banks2[b][:, c0:c1, :], in1=inv[:, c0:c1, :], op=ALU.mult)
+            eng = nc.gpsimd if (ST_ENG == "gpsimd" and b < B - 1) else nc.sync
+            eng.dma_start(out=out[C * b + c0 : C * b + c1].rearrange("c o q -> o c q"), in_=osb[:])
+
+        def ok(n):
+            return 0 <= n < NCH
+
+        for c in range(C):
+            row_mass(c)
+        front_m(0)
+
+        for m in range(NCH + 1):
+            if ok(m):
+                front_v(m)
+            if m == 0:
+                quant_comp()
+            inv_step(2 * (m - 2))
+            if ok(m - 2):
+                for c in range(C):
+                    stage1(m - 2, c)
+            if ok(m - 3):
+                evac(nc.scalar.copy, m - 3, 2)
+                evac(nc.scalar.copy, m - 3, 3)
+            if ok(m):
+                front_s(m, 0)
+            if ok(m - 2):
+                evac(nc.scalar.copy, m - 2, 0)
+                evac(nc.scalar.copy, m - 2, 1)
+            if ok(m):
+                front_s(m, 1)
+            if ok(m - TQ_LAG):
+                quant_t(m - TQ_LAG, 0, C)
+            if ok(m + 1):
+                front_m(m + 1)
+            inv_step(2 * (m - 2) + 1)
+            if ok(m - 1):
+                quant_a(m - 1)
+            n2 = m - TQ_LAG - 1
+            if ok(n2) and n2 % 2 == 1:
+                stage2(n2 // 2, 0, C)
+            n3 = m - F_LAG
+            if ok(n3) and n3 % 2 == 1:
+                final(n3 // 2, 0, C)
+            if ok(m) and m % 2 == 1 and m // 2 + RAWB < B:
+                load(m // 2 + RAWB)
+
+        last = NCH - 1
+        for c in range(C):
+            stage1(last, c)
+        evac(nc.scalar.copy, last - 1, 2)
+        evac(nc.vector.tensor_copy, last - 1, 3)
+        evac(nc.scalar.copy, last, 0)
+        evac(nc.scalar.copy, last, 2)
+        quant_t(last - 2, 0, C)
+        quant_t(last - 1, 0, C)
+        stage2(B - 2, 0, C)
+        final(B - 2, 0, C)
+        evac(nc.vector.tensor_copy, last, 1)
+        quant_t(last, 0, 2)
+        stage2(B - 1, 0, 2)
+        evac(nc.vector.tensor_copy, last, 3)
+        quant_t(last, 2, C)
+        stage2(B - 1, 2, C)
+        final(B - 1, 0, 2)
+        final(B - 1, 2, C)

@@ -16,18 +16,16 @@ H = I // 2
 NCH = 2 * B
 FLOPS = 2 * B * C * O * I * I + 2 * B * C * O * I * O
 
-PIN = False
-SCOLS = [512,512,512,512,416,416,416,416,416,416,416,416,416,416,352,288]
-RAWB = 4
-JH = 3
+SCOLS = [512, 512, 512, 512, 416, 416, 416, 416, 416, 416, 416, 416, 416, 416, 352, 288]
+RAWB = 8
 XE_V = (7,)
 TQ_LAG = 4
-F_LAG = 5
-ST_ENG = "sync"
-PITCH = I + 12
-GP = 4 * PITCH
-DIAG = 4 * (PITCH + 4)
-RAWLEN = GP + H + DIAG
+F_LAG = 6
+DEFER = NCH - 2
+R = 8
+NR = P // R
+PITCH = H + 24
+DIAG = 4 * (PITCH + R)
 
 
 def tile_verticalcompression_t_kernel(tc, a_in, mask, weight, out):
@@ -37,13 +35,13 @@ def tile_verticalcompression_t_kernel(tc, a_in, mask, weight, out):
         rawp = ctx.enter_context(tc.tile_pool(name="rawp", bufs=RAWB))
         grpp = ctx.enter_context(tc.tile_pool(name="grpp", bufs=4))
         acp = ctx.enter_context(tc.tile_pool(name="acp", bufs=4))
-        tgp = ctx.enter_context(tc.tile_pool(name="tgp", bufs=4))
-        tcp = ctx.enter_context(tc.tile_pool(name="tcp", bufs=6))
+        tgp = ctx.enter_context(tc.tile_pool(name="tgp", bufs=6))
+        tcp = ctx.enter_context(tc.tile_pool(name="tcp", bufs=8))
         outp = ctx.enter_context(tc.tile_pool(name="outp", bufs=3))
         ps1 = ctx.enter_context(tc.psum_pool(name="ps1", bufs=7))
         ps2 = ctx.enter_context(tc.psum_pool(name="ps2", bufs=1))
-        if PIN:
-            ctx.enter_context(tc.manual_schedule())
+
+        ctx.enter_context(tc.manual_schedule())
 
         raws = {}
         grps = {}
@@ -53,29 +51,25 @@ def tile_verticalcompression_t_kernel(tc, a_in, mask, weight, out):
         tcs = {}
         banks2 = {}
 
-        def raw_rows(b, g):
-            return raws[b][:, GP * g : GP * (g + 1)].rearrange("p (j w) -> p j w", w=PITCH)
-
-        def load(b):
-            raw = rawp.tile([P, RAWLEN], BF16, tag="raw", name="raw")
-            raws[b] = raw
-            for h in range(2):
-                for g in range(2) if b < JH else [h]:
-                    cols = slice(H * h, H * (h + 1)) if b < JH else slice(0, I)
-                    rows = a_in[b, H * g : H * (g + 1), cols].rearrange("(q j s) w -> s q j w", j=4, s=4)
-                    for s in range(4):
-                        nc.sync.dma_start(
-                            out=raw[s:P:4, GP * g : GP * (g + 1)].rearrange("p (j w) -> p j w", w=PITCH)[:, :, cols],
-                            in_=rows[s],
-                        )
+        def load(n):
+            b, gj = divmod(n, 2)
+            raws[n] = []
+            for g in range(2):
+                raw = rawp.tile([P, DIAG], BF16, tag="raw%d" % g, name="raw", align_bytes=64)
+                raws[n].append(raw)
+                rows = a_in[b, H * g : H * (g + 1), H * gj : H * (gj + 1)].rearrange(
+                    "(r j s) w -> j r s w", j=4, s=R
+                )
+                for j in range(4):
+                    nc.sync.dma_start(out=raw[:, PITCH * j : PITCH * j + H], in_=rows[j])
 
         mask_sb = const.tile([P, I], BF16, name="mask_sb")
         nc.sync.dma_start(out=mask_sb[:], in_=mask)
         w_sb = const.tile([P, C, I], BF16, name="w_sb")
         for c in range(C):
             nc.sync.dma_start(out=w_sb[:, c, :], in_=weight[c])
-        for b in range(RAWB):
-            load(b)
+        for n in range(RAWB):
+            load(n)
 
         ident = const.tile([P, P], BF16, name="ident")
         make_identity(nc, ident[:])
@@ -97,18 +91,21 @@ def tile_verticalcompression_t_kernel(tc, a_in, mask, weight, out):
         inv = const.tile([P, C, P], F32, name="inv")
         for c in range(C):
             nc.vector.tensor_tensor(
-                out=comp[:, c, :, :].rearrange("p t (x s) -> p t x s", s=4),
-                in0=w_sb[:, c, :].rearrange("p (x t s) -> p t x s", t=4, s=4),
-                in1=mask_sb[:].rearrange("p (x t s) -> p t x s", t=4, s=4),
+                out=comp[:, c, :, :].rearrange("p t (x s) -> p t x s", s=R),
+                in0=w_sb[:, c, :].rearrange("p (x t s) -> p t x s", t=4, s=R),
+                in1=mask_sb[:].rearrange("p (x t s) -> p t x s", t=4, s=R),
                 op=ALU.mult,
             )
+        late = []
         for c in range(C):
             for g in range(2):
                 xt = ps1.tile([P, 4, P], BF16, tag="s1", name="xt")
                 for t in range(4):
                     nc.tensor.transpose(xt[:, t, :], comp[:, c, t, P * g : P * (g + 1)], ident[:])
-                fn = nc.vector.tensor_copy if 2 * c + g in XE_V else nc.scalar.copy
-                fn(out=cg[:, g, c, :, :], in_=xt[:].rearrange("p t o -> p o t"))
+                if 2 * c + g in XE_V:
+                    late.append((xt, g, c))
+                else:
+                    nc.scalar.copy(out=cg[:, g, c, :, :], in_=xt[:].rearrange("p t o -> p o t"))
 
         def quant_comp():
             nc.vector.quantize_mx(
@@ -178,39 +175,35 @@ def tile_verticalcompression_t_kernel(tc, a_in, mask, weight, out):
             if 0 <= i < len(inv_steps):
                 inv_steps[i]()
 
-        def zero_diag(b, g):
-            d0 = GP * g + H * g
-            blocks = raws[b][:, d0 : d0 + DIAG].rearrange("p (j u z) -> p j u z", j=4, z=16)[:, :, 0:32, 0:4]
+        def zero_diag(n):
+            blocks = raws[n][n % 2][:].rearrange("p (j u z) -> p j u z", j=4, z=4 * R)[:, :, 0:NR, 0:R]
             nc.vector.tensor_tensor(
                 out=blocks,
                 in0=blocks,
-                in1=noti[:].rearrange("p (q s) -> p q s", s=4).unsqueeze(1).to_broadcast([P, 4, 32, 4]),
+                in1=noti[:].rearrange("p (q s) -> p q s", s=R).unsqueeze(1).to_broadcast([P, 4, NR, R]),
                 op=ALU.mult,
             )
 
-        def regroup(fn, n, g, q0, q1):
-            b, gj = divmod(n, 2)
+        def regroup(fn, n, g, r0, r1):
             fn(
-                out=grps[n][:, g, :, 4 * q0 : 4 * q1, :].rearrange("p t (q s) j -> p q t j s", s=4),
-                in_=raw_rows(b, g)[:, :, H * gj + 16 * q0 : H * gj + 16 * q1].rearrange(
-                    "p j (q t s) -> p q t j s", t=4, s=4
-                ),
+                out=grps[n][:, g, :, R * r0 : R * r1, :].rearrange("p t (r s) j -> p r t j s", s=R),
+                in_=raws[n][g][:, 0 : 4 * PITCH].rearrange("p (j w) -> p j w", w=PITCH)[
+                    :, :, 4 * R * r0 : 4 * R * r1
+                ].rearrange("p j (r t s) -> p r t j s", t=4, s=R),
             )
 
         def front_m(n):
-            zero_diag(n // 2, n % 2)
+            zero_diag(n)
 
         def front_v(n):
-            b, gj = divmod(n, 2)
-            grps[n] = grpp.tile([P, 2, 4, P, 4], BF16, tag="grp", name="grp", align_bytes=64)
-            regroup(nc.vector.tensor_copy, n, gj, 0, 32)
-            if SCOLS[n] < H:
-                regroup(nc.vector.tensor_copy, n, 1 - gj, 0, (H - SCOLS[n]) // 16)
-
-        def front_s(n, piece):
             gj = n % 2
-            if piece == 0:
-                regroup(nc.scalar.copy, n, 1 - gj, (H - SCOLS[n]) // 16, 32)
+            grps[n] = grpp.tile([P, 2, 4, P, 4], BF16, tag="grp", name="grp", align_bytes=64)
+            regroup(nc.vector.tensor_copy, n, gj, 0, NR)
+            if SCOLS[n] < H:
+                regroup(nc.vector.tensor_copy, n, 1 - gj, 0, (H - SCOLS[n]) // (4 * R))
+
+        def front_s(n):
+            regroup(nc.scalar.copy, n, 1 - n % 2, (H - SCOLS[n]) // (4 * R), NR)
 
         def quant_a(n):
             codes = acp.tile([P, 2, H], U32, tag="ac", name="ac", align_bytes=64)
@@ -258,7 +251,10 @@ def tile_verticalcompression_t_kernel(tc, a_in, mask, weight, out):
 
         def stage2(b, c0, c1):
             if c0 == 0:
-                banks2[b] = ps2.tile([P, C, P], F32, tag="s2", name="bank2")
+                if b < B - 1:
+                    banks2[b] = ps2.tile([P, C, P], F32, tag="s2", name="bank2")
+                else:
+                    banks2[b] = ps1.tile([P, C, P], F32, tag="s1", name="bank2")
             for c in range(c0, c1):
                 for gj in range(2):
                     tcod, tscl = tcs[2 * b + gj]
@@ -275,22 +271,28 @@ def tile_verticalcompression_t_kernel(tc, a_in, mask, weight, out):
         def final(b, c0, c1):
             osb = outp.tile([P, c1 - c0, P], F32, tag="osb", name="osb")
             nc.vector.tensor_tensor(out=osb[:], in0=banks2[b][:, c0:c1, :], in1=inv[:, c0:c1, :], op=ALU.mult)
-            eng = nc.gpsimd if (ST_ENG == "gpsimd" and b < B - 1) else nc.sync
-            eng.dma_start(out=out[C * b + c0 : C * b + c1].rearrange("c o q -> o c q"), in_=osb[:])
+            nc.sync.dma_start(out=out[C * b + c0 : C * b + c1].rearrange("c o q -> o c q"), in_=osb[:])
 
         def ok(n):
             return 0 <= n < NCH
 
+        front_m(0)
+        front_v(0)
+        for xt, g, c in late:
+            nc.vector.tensor_copy(out=cg[:, g, c, :, :], in_=xt[:].rearrange("p t o -> p o t"))
         for c in range(C):
             row_mass(c)
-        front_m(0)
+        quant_comp()
+        front_s(0)
+        front_m(1)
 
-        for m in range(NCH + 1):
+        for m in range(1, NCH + 1):
             if ok(m):
                 front_v(m)
-            if m == 0:
-                quant_comp()
             inv_step(2 * (m - 2))
+            n3 = m - F_LAG
+            if ok(n3) and n3 % 2 == 1:
+                final(n3 // 2, 0, C)
             if ok(m - 2):
                 for c in range(C):
                     stage1(m - 2, c)
@@ -298,13 +300,11 @@ def tile_verticalcompression_t_kernel(tc, a_in, mask, weight, out):
                 evac(nc.scalar.copy, m - 3, 2)
                 evac(nc.scalar.copy, m - 3, 3)
             if ok(m):
-                front_s(m, 0)
+                front_s(m)
             if ok(m - 2):
                 evac(nc.scalar.copy, m - 2, 0)
                 evac(nc.scalar.copy, m - 2, 1)
-            if ok(m):
-                front_s(m, 1)
-            if ok(m - TQ_LAG):
+            if ok(m - TQ_LAG) and m < DEFER:
                 quant_t(m - TQ_LAG, 0, C)
             if ok(m + 1):
                 front_m(m + 1)
@@ -312,29 +312,32 @@ def tile_verticalcompression_t_kernel(tc, a_in, mask, weight, out):
             if ok(m - 1):
                 quant_a(m - 1)
             n2 = m - TQ_LAG - 1
-            if ok(n2) and n2 % 2 == 1:
+            if ok(n2) and n2 % 2 == 1 and m <= DEFER:
                 stage2(n2 // 2, 0, C)
-            n3 = m - F_LAG
-            if ok(n3) and n3 % 2 == 1:
-                final(n3 // 2, 0, C)
-            if ok(m) and m % 2 == 1 and m // 2 + RAWB < B:
-                load(m // 2 + RAWB)
+            if m - 1 + RAWB < NCH:
+                load(m - 1 + RAWB)
 
         last = NCH - 1
-        for c in range(C):
-            stage1(last, c)
+        stage1(last, 0)
+        stage1(last, 1)
         evac(nc.scalar.copy, last - 1, 2)
-        evac(nc.vector.tensor_copy, last - 1, 3)
         evac(nc.scalar.copy, last, 0)
+        for n in range(DEFER - TQ_LAG, last - 1):
+            quant_t(n, 0, C)
+            if n == last - 3:
+                evac(nc.vector.tensor_copy, last - 1, 3)
+        stage2(B - 3, 0, C)
+        final(B - 3, 0, C)
+        stage1(last, 2)
+        stage1(last, 3)
+        evac(nc.vector.tensor_copy, last, 1)
         evac(nc.scalar.copy, last, 2)
-        quant_t(last - 2, 0, C)
         quant_t(last - 1, 0, C)
         stage2(B - 2, 0, C)
-        final(B - 2, 0, C)
-        evac(nc.vector.tensor_copy, last, 1)
         quant_t(last, 0, 2)
         stage2(B - 1, 0, 2)
         evac(nc.vector.tensor_copy, last, 3)
+        final(B - 2, 0, C)
         quant_t(last, 2, C)
         stage2(B - 1, 2, C)
         final(B - 1, 0, 2)

@@ -22,11 +22,8 @@ XE_V = (7,)
 TQ_LAG = 4
 F_LAG = 6
 DEFER = NCH - 2
-R = 8
+R = 4
 NR = P // R
-PITCH = H + 24
-DIAG = 4 * (PITCH + R)
-
 
 def tile_verticalcompression_t_kernel(tc, a_in, mask, weight, out):
     nc = tc.nc
@@ -55,13 +52,13 @@ def tile_verticalcompression_t_kernel(tc, a_in, mask, weight, out):
             b, gj = divmod(n, 2)
             raws[n] = []
             for g in range(2):
-                raw = rawp.tile([P, DIAG], BF16, tag="raw%d" % g, name="raw", align_bytes=64)
+                raw = rawp.tile([P, 4, H], BF16, tag="raw%d" % g, name="raw", align_bytes=64)
                 raws[n].append(raw)
                 rows = a_in[b, H * g : H * (g + 1), H * gj : H * (gj + 1)].rearrange(
                     "(r j s) w -> j r s w", j=4, s=R
                 )
                 for j in range(4):
-                    nc.sync.dma_start(out=raw[:, PITCH * j : PITCH * j + H], in_=rows[j])
+                    nc.sync.dma_start(out=raw[:, j, :], in_=rows[j])
 
         mask_sb = const.tile([P, I], BF16, name="mask_sb")
         nc.sync.dma_start(out=mask_sb[:], in_=mask)
@@ -79,6 +76,12 @@ def tile_verticalcompression_t_kernel(tc, a_in, mask, weight, out):
         nc.vector.tensor_scalar(
             out=noti[:], in0=ident[:], scalar1=-1.0, scalar2=1.0, op0=ALU.mult, op1=ALU.add
         )
+        off = const.tile([P, 2, NR, 2 * R], BF16, name="off", align_bytes=64)
+        nc.gpsimd.memset(off[:], 1.0)
+        for e in range(2):
+            nc.vector.tensor_copy(
+                out=off[:, e, :, R * e : R * (e + 1)], in_=noti[:].rearrange("p (r s) -> p r s", s=R)
+            )
 
         comp = const.tile([P, C, 4, I // 4], BF16, name="comp")
         cg = const.tile([P, 2, C, P, 4], BF16, name="cg", align_bytes=64)
@@ -176,20 +179,17 @@ def tile_verticalcompression_t_kernel(tc, a_in, mask, weight, out):
                 inv_steps[i]()
 
         def zero_diag(n):
-            blocks = raws[n][n % 2][:].rearrange("p (j u z) -> p j u z", j=4, z=4 * R)[:, :, 0:NR, 0:R]
-            nc.vector.tensor_tensor(
-                out=blocks,
-                in0=blocks,
-                in1=noti[:].rearrange("p (q s) -> p q s", s=R).unsqueeze(1).to_broadcast([P, 4, NR, R]),
-                op=ALU.mult,
-            )
+            raw = raws[n][n % 2]
+            for h in range(2):
+                blocks = raw[:, 2 * h : 2 * h + 2, :].rearrange("p e (r z) -> p e r z", z=4 * R)[
+                    :, :, :, 2 * R * h : 2 * R * (h + 1)
+                ]
+                nc.vector.tensor_tensor(out=blocks, in0=blocks, in1=off[:], op=ALU.mult)
 
         def regroup(fn, n, g, r0, r1):
             fn(
                 out=grps[n][:, g, :, R * r0 : R * r1, :].rearrange("p t (r s) j -> p r t j s", s=R),
-                in_=raws[n][g][:, 0 : 4 * PITCH].rearrange("p (j w) -> p j w", w=PITCH)[
-                    :, :, 4 * R * r0 : 4 * R * r1
-                ].rearrange("p j (r t s) -> p r t j s", t=4, s=R),
+                in_=raws[n][g][:, :, 4 * R * r0 : 4 * R * r1].rearrange("p j (r t s) -> p r t j s", t=4, s=R),
             )
 
         def front_m(n):

@@ -16,11 +16,11 @@ H = I // 2
 NCH = 2 * B
 FLOPS = 2 * B * C * O * I * I + 2 * B * C * O * I * O
 
-SCOLS = [512, 512, 512, 512, 416, 416, 416, 416, 416, 416, 416, 416, 416, 416, 352, 288]
+SCOLS = [512, 512, 512, 512, 320, 512, 320, 512, 320, 512, 320, 512, 320, 512, 320, 288]
 RAWB = 8
 XE_V = (7,)
 TQ_LAG = 4
-F_LAG = 6
+F_LAG = 7
 DEFER = NCH - 2
 R = 4
 NR = P // R
@@ -32,8 +32,8 @@ def tile_verticalcompression_t_kernel(tc, a_in, mask, weight, out):
         rawp = ctx.enter_context(tc.tile_pool(name="rawp", bufs=RAWB))
         grpp = ctx.enter_context(tc.tile_pool(name="grpp", bufs=4))
         acp = ctx.enter_context(tc.tile_pool(name="acp", bufs=4))
-        tgp = ctx.enter_context(tc.tile_pool(name="tgp", bufs=6))
-        tcp = ctx.enter_context(tc.tile_pool(name="tcp", bufs=8))
+        tgp = ctx.enter_context(tc.tile_pool(name="tgp", bufs=4))
+        tcp = ctx.enter_context(tc.tile_pool(name="tcp", bufs=4))
         outp = ctx.enter_context(tc.tile_pool(name="outp", bufs=3))
         ps1 = ctx.enter_context(tc.psum_pool(name="ps1", bufs=7))
         ps2 = ctx.enter_context(tc.psum_pool(name="ps2", bufs=1))
@@ -132,7 +132,6 @@ def tile_verticalcompression_t_kernel(tc, a_in, mask, weight, out):
         safe = const.tile([P, C], F32, name="safe")
         rec = const.tile([P, C], F32, name="rec")
         rp = const.tile([P, C], F32, name="rp")
-        spread = const.tile([P, C, P], F32, name="spread")
         prod = const.tile([P, C, P], F32, name="prod")
 
         def inv_rs():
@@ -152,10 +151,9 @@ def tile_verticalcompression_t_kernel(tc, a_in, mask, weight, out):
             )
 
         def inv_spread():
-            nc.vector.tensor_copy(out=spread[:], in_=rp[:].unsqueeze(2).to_broadcast([P, C, P]))
             rsbs[1] = ps2.tile([P, C, P], F32, tag="s2", name="rb")
             for c in range(C):
-                nc.tensor.transpose(rsbs[1][:, c, :], spread[:, c, :], identf[:])
+                nc.tensor.transpose(rsbs[1][:, c, :], rp[:, c : c + 1].to_broadcast([P, P]), identf[:])
 
         def inv_prod():
             nc.vector.tensor_tensor(
@@ -233,20 +231,21 @@ def tile_verticalcompression_t_kernel(tc, a_in, mask, weight, out):
 
         def evac(fn, n, c):
             if c == 0:
-                tgs[n] = tgp.tile([P, C, P, 4], BF16, tag="tg", name="tg", align_bytes=64)
-            fn(out=tgs[n][:, c, :, :], in_=banks[(n, c)][:].rearrange("p t o -> p o t"))
+                if n % 2 == 0:
+                    tgs[n // 2] = tgp.tile([P, 2, C, P, 4], BF16, tag="tg", name="tg", align_bytes=64)
+            fn(out=tgs[n // 2][:, n % 2, c, :, :], in_=banks[(n, c)][:].rearrange("p t o -> p o t"))
 
-        def quant_t(n, c0, c1):
-            if c0 == 0:
-                tcs[n] = (
-                    tcp.tile([P, C, P], U32, tag="tcod", name="tcod", align_bytes=64),
-                    tcp.tile([P, C, P], U8, tag="tscl", name="tscl", align_bytes=64),
+        def quant_t(b, i0, i1):
+            if i0 == 0:
+                tcs[b] = (
+                    tcp.tile([P, 2 * C, P], U32, tag="tcod", name="tcod", align_bytes=64),
+                    tcp.tile([P, 2 * C, P], U8, tag="tscl", name="tscl", align_bytes=64),
                 )
-            tcod, tscl = tcs[n]
+            tcod, tscl = tcs[b]
             nc.vector.quantize_mx(
-                out=tcod[:, c0:c1, :].rearrange("p c o -> p (c o)").bitcast(FP8X4),
-                scales=tscl[:, c0:c1, :].rearrange("p c o -> p (c o)"),
-                in_=tgs[n][:, c0:c1, :, :].rearrange("p c o t -> p (c o t)"),
+                out=tcod[:, i0:i1, :].rearrange("p i o -> p (i o)").bitcast(FP8X4),
+                scales=tscl[:, i0:i1, :].rearrange("p i o -> p (i o)"),
+                in_=tgs[b][:].rearrange("p g c o t -> p (g c) (o t)")[:, i0:i1, :].rearrange("p i x -> p (i x)"),
             )
 
         def stage2(b, c0, c1):
@@ -257,11 +256,11 @@ def tile_verticalcompression_t_kernel(tc, a_in, mask, weight, out):
                     banks2[b] = ps1.tile([P, C, P], F32, tag="s1", name="bank2")
             for c in range(c0, c1):
                 for gj in range(2):
-                    tcod, tscl = tcs[2 * b + gj]
+                    tcod, tscl = tcs[b]
                     nc.tensor.matmul_mx(
                         out=banks2[b][:, c, :],
-                        lhsT=tcod[:, c, :].bitcast(FP8X4),
-                        lhsT_scale=tscl[:, c, :],
+                        lhsT=tcod[:, C * gj + c, :].bitcast(FP8X4),
+                        lhsT_scale=tscl[:, C * gj + c, :],
                         rhs=ccodes[:, gj, c, :].bitcast(FP8X4),
                         rhs_scale=cscales[:, gj, c, :],
                         start=(gj == 0),
@@ -304,8 +303,8 @@ def tile_verticalcompression_t_kernel(tc, a_in, mask, weight, out):
             if ok(m - 2):
                 evac(nc.scalar.copy, m - 2, 0)
                 evac(nc.scalar.copy, m - 2, 1)
-            if ok(m - TQ_LAG) and m < DEFER:
-                quant_t(m - TQ_LAG, 0, C)
+            if ok(m - TQ_LAG) and m < DEFER and (m - TQ_LAG) % 2 == 1:
+                quant_t((m - TQ_LAG) // 2, 0, 2 * C)
             if ok(m + 1):
                 front_m(m + 1)
             inv_step(2 * (m - 2) + 1)
@@ -321,24 +320,23 @@ def tile_verticalcompression_t_kernel(tc, a_in, mask, weight, out):
         stage1(last, 0)
         stage1(last, 1)
         evac(nc.scalar.copy, last - 1, 2)
+        evac(nc.scalar.copy, last - 1, 3)
         evac(nc.scalar.copy, last, 0)
-        for n in range(DEFER - TQ_LAG, last - 1):
-            quant_t(n, 0, C)
-            if n == last - 3:
-                evac(nc.vector.tensor_copy, last - 1, 3)
+        quant_t(B - 3, 0, 2 * C)
+        quant_t(B - 2, 0, 2 * C)
         stage2(B - 3, 0, C)
         final(B - 3, 0, C)
         stage1(last, 2)
         stage1(last, 3)
-        evac(nc.vector.tensor_copy, last, 1)
+        evac(nc.scalar.copy, last, 1)
         evac(nc.scalar.copy, last, 2)
-        quant_t(last - 1, 0, C)
+        quant_t(B - 1, 0, C)
         stage2(B - 2, 0, C)
-        quant_t(last, 0, 2)
-        stage2(B - 1, 0, 2)
         evac(nc.vector.tensor_copy, last, 3)
-        final(B - 2, 0, C)
-        quant_t(last, 2, C)
+        quant_t(B - 1, C, C + 2)
+        stage2(B - 1, 0, 2)
+        quant_t(B - 1, C + 2, 2 * C)
         stage2(B - 1, 2, C)
+        final(B - 2, 0, C)
         final(B - 1, 0, 2)
         final(B - 1, 2, C)

@@ -16,7 +16,8 @@ H = I // 2
 NCH = 2 * B
 FLOPS = 2 * B * C * O * I * I + 2 * B * C * O * I * O
 
-SCOLS = [512, 512, 512, 512, 320, 512, 320, 512, 320, 512, 320, 512, 320, 512, 320, 288]
+XR = 8
+SR = [24, 24, 24, 24, 18, 24, 18, 24, 18, 24, 18, 24, 18, 24, 18, 14]
 RAWB = 8
 XE_V = (7,)
 TQ_LAG = 4
@@ -42,6 +43,7 @@ def tile_verticalcompression_t_kernel(tc, a_in, mask, weight, out):
 
         raws = {}
         grps = {}
+        xbs = {}
         acs = {}
         banks = {}
         tgs = {}
@@ -197,11 +199,26 @@ def tile_verticalcompression_t_kernel(tc, a_in, mask, weight, out):
             gj = n % 2
             grps[n] = grpp.tile([P, 2, 4, P, 4], BF16, tag="grp", name="grp", align_bytes=64)
             regroup(nc.vector.tensor_copy, n, gj, 0, NR)
-            if SCOLS[n] < H:
-                regroup(nc.vector.tensor_copy, n, 1 - gj, 0, (H - SCOLS[n]) // (4 * R))
+            if XR + SR[n] < NR:
+                regroup(nc.vector.tensor_copy, n, 1 - gj, XR + SR[n], NR)
 
         def front_s(n):
-            regroup(nc.scalar.copy, n, 1 - n % 2, (H - SCOLS[n]) // (4 * R), NR)
+            g = 1 - n % 2
+            nc.scalar.copy(
+                out=grps[n][:, g, :, 0 : R * XR, :].rearrange("p t (r s) j -> p r t (s j)", s=R),
+                in_=xbs[n][:].rearrange("p (r t x) -> p r t x", t=4, x=4 * R),
+            )
+            regroup(nc.scalar.copy, n, g, XR, XR + SR[n])
+
+        def lay_out(n):
+            xbs[n] = ps1.tile([P, XR * 4 * 4 * R], BF16, tag="s1", name="xb")
+            nc.tensor.matmul(
+                out=xbs[n][:].rearrange("p (w j) -> p j w", j=4),
+                lhsT=ident[:],
+                rhs=raws[n][1 - n % 2][:, :, 0 : 4 * R * XR],
+                start=True,
+                stop=True,
+            )
 
         def quant_a(n):
             codes = acp.tile([P, 2, H], U32, tag="ac", name="ac", align_bytes=64)
@@ -275,6 +292,7 @@ def tile_verticalcompression_t_kernel(tc, a_in, mask, weight, out):
         def ok(n):
             return 0 <= n < NCH
 
+        lay_out(0)
         front_m(0)
         front_v(0)
         for xt, g, c in late:
@@ -283,6 +301,7 @@ def tile_verticalcompression_t_kernel(tc, a_in, mask, weight, out):
             row_mass(c)
         quant_comp()
         front_s(0)
+        lay_out(1)
         front_m(1)
 
         for m in range(1, NCH + 1):
@@ -313,6 +332,8 @@ def tile_verticalcompression_t_kernel(tc, a_in, mask, weight, out):
             n2 = m - TQ_LAG - 1
             if ok(n2) and n2 % 2 == 1 and m <= DEFER:
                 stage2(n2 // 2, 0, C)
+            if ok(m + 1):
+                lay_out(m + 1)
             if m - 1 + RAWB < NCH:
                 load(m - 1 + RAWB)
 

@@ -16,8 +16,8 @@ H = I // 2
 NCH = 2 * B
 FLOPS = 2 * B * C * O * I * I + 2 * B * C * O * I * O
 
-XR = 8
-SR = [24, 24, 24, 24, 18, 24, 18, 24, 18, 24, 18, 24, 18, 24, 18, 14]
+XR = 12
+SR = [20] * 14 + [16, 12]
 RAWB = 8
 XE_V = (7,)
 TQ_LAG = 4
@@ -212,13 +212,15 @@ def tile_verticalcompression_t_kernel(tc, a_in, mask, weight, out):
 
         def lay_out(n):
             xbs[n] = ps1.tile([P, XR * 4 * 4 * R], BF16, tag="s1", name="xb")
-            nc.tensor.matmul(
-                out=xbs[n][:].rearrange("p (w j) -> p j w", j=4),
-                lhsT=ident[:],
-                rhs=raws[n][1 - n % 2][:, :, 0 : 4 * R * XR],
-                start=True,
-                stop=True,
-            )
+            half = 2 * R * XR
+            for w0 in (0, half):
+                nc.tensor.matmul(
+                    out=xbs[n][:, 4 * w0 : 4 * (w0 + half)].rearrange("p (w j) -> p j w", j=4),
+                    lhsT=ident[:],
+                    rhs=raws[n][1 - n % 2][:, :, w0 : w0 + half],
+                    start=True,
+                    stop=True,
+                )
 
         def quant_a(n):
             codes = acp.tile([P, 2, H], U32, tag="ac", name="ac", align_bytes=64)

@@ -52,10 +52,10 @@ def tile_verticalcompression_t_kernel(tc, a_in, mask, weight, out):
 
         def load(n):
             b, gj = divmod(n, 2)
-            raws[n] = []
-            for g in range(2):
+            raws[n] = {}
+            for g in (gj, 1 - gj):
                 raw = rawp.tile([P, 4, H], BF16, tag="raw%d" % g, name="raw", align_bytes=64)
-                raws[n].append(raw)
+                raws[n][g] = raw
                 rows = a_in[b, H * g : H * (g + 1), H * gj : H * (gj + 1)].rearrange(
                     "(r j s) w -> j r s w", j=4, s=R
                 )
@@ -329,6 +329,8 @@ def tile_verticalcompression_t_kernel(tc, a_in, mask, weight, out):
             if ok(m + 1):
                 front_m(m + 1)
             inv_step(2 * (m - 2) + 1)
+            if m == NCH:
+                quant_t(B - 3, 0, 2 * C)
             if ok(m - 1):
                 quant_a(m - 1)
             n2 = m - TQ_LAG - 1
@@ -345,7 +347,6 @@ def tile_verticalcompression_t_kernel(tc, a_in, mask, weight, out):
         evac(nc.scalar.copy, last - 1, 2)
         evac(nc.scalar.copy, last - 1, 3)
         evac(nc.scalar.copy, last, 0)
-        quant_t(B - 3, 0, 2 * C)
         quant_t(B - 2, 0, 2 * C)
         stage2(B - 3, 0, C)
         final(B - 3, 0, C)

from contextlib import ExitStack

import concourse.mybir as mybir
from concourse.masks import make_identity

F32 = mybir.dt.float32
BF16 = mybir.dt.bfloat16
U32 = mybir.dt.uint32
U8 = mybir.dt.uint8
FP8X4 = mybir.dt.float8_e4m3fn_x4
ALU = mybir.AluOpType

P = 128
B, I, O, C = 8, 1024, 128, 4
H = I // 2
NCH = 2 * B
FLOPS = 2 * B * C * O * I * I + 2 * B * C * O * I * O

XR = 12
SR = [20] * 14 + [16, 12]
RAWB = 8
XE_V = (7,)
TQ_LAG = 4
F_LAG = 7
DEFER = NCH - 2
R = 4
NR = P // R

def tile_verticalcompression_t_kernel(tc, a_in, mask, weight, out):
    nc = tc.nc
    with ExitStack() as ctx:
        const = ctx.enter_context(tc.tile_pool(name="const", bufs=1))
        rawp = ctx.enter_context(tc.tile_pool(name="rawp", bufs=RAWB))
        grpp = ctx.enter_context(tc.tile_pool(name="grpp", bufs=4))
        acp = ctx.enter_context(tc.tile_pool(name="acp", bufs=4))
        tgp = ctx.enter_context(tc.tile_pool(name="tgp", bufs=4))
        tcp = ctx.enter_context(tc.tile_pool(name="tcp", bufs=4))
        outp = ctx.enter_context(tc.tile_pool(name="outp", bufs=3))
        ps1 = ctx.enter_context(tc.psum_pool(name="ps1", bufs=7))
        ps2 = ctx.enter_context(tc.psum_pool(name="ps2", bufs=1))

        ctx.enter_context(tc.manual_schedule())

        raws = {}
        grps = {}
        xbs = {}
        acs = {}
        banks = {}
        tgs = {}
        tcs = {}
        banks2 = {}

        def load(n):
            b, gj = divmod(n, 2)
            raws[n] = {}
            for g in (gj, 1 - gj):
                raw = rawp.tile([P, 4, H], BF16, tag="raw%d" % g, name="raw", align_bytes=64)
                raws[n][g] = raw
                rows = a_in[b, H * g : H * (g + 1), H * gj : H * (gj + 1)].rearrange(
                    "(r j s) w -> j r s w", j=4, s=R
                )
                for j in range(4):
                    nc.sync.dma_start(out=raw[:, j, :], in_=rows[j])

        mask_sb = const.tile([P, I], BF16, name="mask_sb")
        nc.sync.dma_start(out=mask_sb[:], in_=mask)
        w_sb = const.tile([P, C, I], BF16, name="w_sb")
        for c in range(C):
            nc.sync.dma_start(out=w_sb[:, c, :], in_=weight[c])
        for n in range(RAWB):
            load(n)

        ident = const.tile([P, P], BF16, name="ident")
        make_identity(nc, ident[:])
        identf = const.tile([P, P], F32, name="identf")
        make_identity(nc, identf[:])
        noti = const.tile([P, P], BF16, name="noti")
        nc.vector.tensor_scalar(
            out=noti[:], in0=ident[:], scalar1=-1.0, scalar2=1.0, op0=ALU.mult, op1=ALU.add
        )
        off = const.tile([P, 2, NR, 2 * R], BF16, name="off", align_bytes=64)
        nc.gpsimd.memset(off[:], 1.0)
        for e in range(2):
            nc.vector.tensor_copy(
                out=off[:, e, :, R * e : R * (e + 1)], in_=noti[:].rearrange("p (r s) -> p r s", s=R)
            )

        comp = const.tile([P, C, 4, I // 4], BF16, name="comp")
        cg = const.tile([P, 2, C, P, 4], BF16, name="cg", align_bytes=64)
        ccodes = const.tile([P, 2, C, P], U32, name="ccodes", align_bytes=64)
        cscales = const.tile([P, 2, C, P], U8, name="cscales", align_bytes=64)
        rs = const.tile([P, C], F32, name="rs")
        ones = const.tile([P, 32], BF16, name="ones")
        nc.gpsimd.memset(ones[:], 1.0)
        rsbs = {}
        inv = const.tile([P, C, P], F32, name="inv")
        for c in range(C):
            nc.vector.tensor_tensor(
                out=comp[:, c, :, :].rearrange("p t (x s) -> p t x s", s=R),
                in0=w_sb[:, c, :].rearrange("p (x t s) -> p t x s", t=4, s=R),
                in1=mask_sb[:].rearrange("p (x t s) -> p t x s", t=4, s=R),
                op=ALU.mult,
            )
        late = []
        for c in range(C):
            for g in range(2):
                xt = ps1.tile([P, 4, P], BF16, tag="s1", name="xt")
                for t in range(4):
                    nc.tensor.transpose(xt[:, t, :], comp[:, c, t, P * g : P * (g + 1)], ident[:])
                if 2 * c + g in XE_V:
                    late.append((xt, g, c))
                else:
                    nc.scalar.copy(out=cg[:, g, c, :, :], in_=xt[:].rearrange("p t o -> p o t"))

        def quant_comp():
            nc.vector.quantize_mx(
                out=ccodes[:].rearrange("p g c o -> p (g c o)").bitcast(FP8X4),
                scales=cscales[:].rearrange("p g c o -> p (g c o)"),
                in_=cg[:].rearrange("p g c o t -> p (g c o t)"),
            )

        def row_mass(c):
            if c == 0:
                rsbs[0] = ps2.tile([P, C, 32], F32, tag="s2", name="rsb")
            for i in range(8):
                nc.tensor.matmul(
                    out=rsbs[0][:, c, :],
                    lhsT=cg[:, i // 4, c, :, i % 4],
                    rhs=ones[:],
                    start=(i == 0),
                    stop=(i == 7),
                )

        safe = const.tile([P, C], F32, name="safe")
        rec = const.tile([P, C], F32, name="rec")
        rp = const.tile([P, C], F32, name="rp")
        prod = const.tile([P, C, P], F32, name="prod")

        def inv_rs():
            nc.vector.tensor_copy(out=rs[:], in_=rsbs[0][:, :, 0])

        def inv_safe():
            nc.vector.scalar_tensor_tensor(
                out=safe[:], in0=rs[:], scalar=0.0, in1=rs[:], op0=ALU.is_equal, op1=ALU.add
            )

        def inv_rec():
            nc.vector.reciprocal(out=rec[:], in_=safe[:])

        def inv_rp():
            nc.vector.scalar_tensor_tensor(
                out=rp[:], in0=rs[:], scalar=0.0, in1=rec[:], op0=ALU.not_equal, op1=ALU.mult
            )

        def inv_spread():
            rsbs[1] = ps2.tile([P, C, P], F32, tag="s2", name="rb")
            for c in range(C):
                nc.tensor.transpose(rsbs[1][:, c, :], rp[:, c : c + 1].to_broadcast([P, P]), identf[:])

        def inv_prod():
            nc.vector.tensor_tensor(
                out=prod[:], in0=rsbs[1][:], in1=rp[:].unsqueeze(2).to_broadcast([P, C, P]), op=ALU.mult
            )

        def inv_fix():
            nc.vector.scalar_tensor_tensor(
                out=inv[:].rearrange("p c o -> p (c o)"),
                in0=prod[:].rearrange("p c o -> p (c o)"),
                scalar=0.0,
                in1=prod[:].rearrange("p c o -> p (c o)"),
                op0=ALU.is_equal,
                op1=ALU.add,
            )

        inv_steps = [inv_rs, inv_safe, inv_rec, inv_rp, inv_spread, inv_prod, inv_fix]

        def inv_step(i):
            if 0 <= i < len(inv_steps):
                inv_steps[i]()

        def zero_diag(n):
            raw = raws[n][n % 2]
            for h in range(2):
                blocks = raw[:, 2 * h : 2 * h + 2, :].rearrange("p e (r z) -> p e r z", z=4 * R)[
                    :, :, :, 2 * R * h : 2 * R * (h + 1)
                ]
                nc.vector.tensor_tensor(out=blocks, in0=blocks, in1=off[:], op=ALU.mult)

        def regroup(fn, n, g, r0, r1):
            fn(
                out=grps[n][:, g, :, R * r0 : R * r1, :].rearrange("p t (r s) j -> p r t j s", s=R),
                in_=raws[n][g][:, :, 4 * R * r0 : 4 * R * r1].rearrange("p j (r t s) -> p r t j s", t=4, s=R),
            )

        def front_m(n):
            zero_diag(n)

        def front_v(n):
            gj = n % 2
            grps[n] = grpp.tile([P, 2, 4, P, 4], BF16, tag="grp", name="grp", align_bytes=64)
            regroup(nc.vector.tensor_copy, n, gj, 0, NR)
            if XR + SR[n] < NR:
                regroup(nc.vector.tensor_copy, n, 1 - gj, XR + SR[n], NR)

        def front_s(n):
            g = 1 - n % 2
            nc.scalar.copy(
                out=grps[n][:, g, :, 0 : R * XR, :].rearrange("p t (r s) j -> p r t (s j)", s=R),
                in_=xbs[n][:].rearrange("p (r t x) -> p r t x", t=4, x=4 * R),
            )
            regroup(nc.scalar.copy, n, g, XR, XR + SR[n])

        def lay_out(n):
            xbs[n] = ps1.tile([P, XR * 4 * 4 * R], BF16, tag="s1", name="xb")
            half = 2 * R * XR
            for w0 in (0, half):
                nc.tensor.matmul(
                    out=xbs[n][:, 4 * w0 : 4 * (w0 + half)].rearrange("p (w j) -> p j w", j=4),
                    lhsT=ident[:],
                    rhs=raws[n][1 - n % 2][:, :, w0 : w0 + half],
                    start=True,
                    stop=True,
                )

        def quant_a(n):
            codes = acp.tile([P, 2, H], U32, tag="ac", name="ac", align_bytes=64)
            scl = acp.tile([P, 2, H], U8, tag="asc", name="asc", align_bytes=64)
            nc.vector.quantize_mx(
                out=codes[:].rearrange("p g w -> p (g w)").bitcast(FP8X4),
                scales=scl[:].rearrange("p g w -> p (g w)"),
                in_=grps[n][:].rearrange("p g t m j -> p (g t m j)"),
            )
            acs[n] = (codes, scl)

        def stage1(n, c):
            codes, scl = acs[n]
            bank = ps1.tile([P, 4, P], F32, tag="s1", name="bank")
            for t in range(4):
                for g in range(2):
                    nc.tensor.matmul_mx(
                        out=bank[:, t, :],
                        lhsT=codes[:, g, P * t : P * (t + 1)].bitcast(FP8X4),
                        lhsT_scale=scl[:, g, P * t : P * (t + 1)],
                        rhs=ccodes[:, g, c, :].bitcast(FP8X4),
                        rhs_scale=cscales[:, g, c, :],
                        start=(g == 0),
                        stop=(g == 1),
                    )
            banks[(n, c)] = bank

        def evac(fn, n, c):
            if c == 0:
                if n % 2 == 0:
                    tgs[n // 2] = tgp.tile([P, 2, C, P, 4], BF16, tag="tg", name="tg", align_bytes=64)
            fn(out=tgs[n // 2][:, n % 2, c, :, :], in_=banks[(n, c)][:].rearrange("p t o -> p o t"))

        def quant_t(b, i0, i1):
            if i0 == 0:
                tcs[b] = (
                    tcp.tile([P, 2 * C, P], U32, tag="tcod", name="tcod", align_bytes=64),
                    tcp.tile([P, 2 * C, P], U8, tag="tscl", name="tscl", align_bytes=64),
                )
            tcod, tscl = tcs[b]
            nc.vector.quantize_mx(
                out=tcod[:, i0:i1, :].rearrange("p i o -> p (i o)").bitcast(FP8X4),
                scales=tscl[:, i0:i1, :].rearrange("p i o -> p (i o)"),
                in_=tgs[b][:].rearrange("p g c o t -> p (g c) (o t)")[:, i0:i1, :].rearrange("p i x -> p (i x)"),
            )

        def stage2(b, c0, c1):
            if c0 == 0:
                if b < B - 1:
                    banks2[b] = ps2.tile([P, C, P], F32, tag="s2", name="bank2")
                else:
                    banks2[b] = ps1.tile([P, C, P], F32, tag="s1", name="bank2")
            for c in range(c0, c1):
                for gj in range(2):
                    tcod, tscl = tcs[b]
                    nc.tensor.matmul_mx(
                        out=banks2[b][:, c, :],
                        lhsT=tcod[:, C * gj + c, :].bitcast(FP8X4),
                        lhsT_scale=tscl[:, C * gj + c, :],
                        rhs=ccodes[:, gj, c, :].bitcast(FP8X4),
                        rhs_scale=cscales[:, gj, c, :],
                        start=(gj == 0),
                        stop=(gj == 1),
                    )

        def final(b, c0, c1):
            osb = outp.tile([P, c1 - c0, P], F32, tag="osb", name="osb")
            nc.vector.tensor_tensor(out=osb[:], in0=banks2[b][:, c0:c1, :], in1=inv[:, c0:c1, :], op=ALU.mult)
            nc.sync.dma_start(out=out[C * b + c0 : C * b + c1].rearrange("c o q -> o c q"), in_=osb[:])

        def ok(n):
            return 0 <= n < NCH

        lay_out(0)
        front_m(0)
        front_v(0)
        for xt, g, c in late:
            nc.vector.tensor_copy(out=cg[:, g, c, :, :], in_=xt[:].rearrange("p t o -> p o t"))
        for c in range(C):
            row_mass(c)
        quant_comp()
        front_s(0)
        lay_out(1)
        front_m(1)

        for m in range(1, NCH + 1):
            if ok(m):
                front_v(m)
            inv_step(2 * (m - 2))
            n3 = m - F_LAG
            if ok(n3) and n3 % 2 == 1:
                final(n3 // 2, 0, C)
            if ok(m - 2):
                for c in range(C):
                    stage1(m - 2, c)
            if ok(m - 3):
                evac(nc.scalar.copy, m - 3, 2)
                evac(nc.scalar.copy, m - 3, 3)
            if ok(m):
                front_s(m)
            if ok(m - 2):
                evac(nc.scalar.copy, m - 2, 0)
                evac(nc.scalar.copy, m - 2, 1)
            if ok(m - TQ_LAG) and m < DEFER and (m - TQ_LAG) % 2 == 1:
                quant_t((m - TQ_LAG) // 2, 0, 2 * C)
            if ok(m + 1):
                front_m(m + 1)
            inv_step(2 * (m - 2) + 1)
            if m == NCH:
                quant_t(B - 3, 0, 2 * C)
            if ok(m - 1):
                quant_a(m - 1)
            n2 = m - TQ_LAG - 1
            if ok(n2) and n2 % 2 == 1 and m <= DEFER:
                stage2(n2 // 2, 0, C)
            if ok(m + 1):
                lay_out(m + 1)
            if m - 1 + RAWB < NCH:
                load(m - 1 + RAWB)

        last = NCH - 1
        stage1(last, 0)
        stage1(last, 1)
        evac(nc.scalar.copy, last - 1, 2)
        evac(nc.scalar.copy, last - 1, 3)
        evac(nc.scalar.copy, last, 0)
        quant_t(B - 2, 0, 2 * C)
        stage2(B - 3, 0, C)
        final(B - 3, 0, C)
        stage1(last, 2)
        stage1(last, 3)
        evac(nc.scalar.copy, last, 1)
        evac(nc.scalar.copy, last, 2)
        quant_t(B - 1, 0, C)
        stage2(B - 2, 0, C)
        evac(nc.vector.tensor_copy, last, 3)
        quant_t(B - 1, C, C + 2)
        stage2(B - 1, 0, 2)
        quant_t(B - 1, C + 2, 2 * C)
        stage2(B - 1, 2, C)
        final(B - 2, 0, C)
        final(B - 1, 0, 2)
        final(B - 1, 2, C)
